import numpy as np
import ml_dtypes


def mxq(x, axis, fmt="e4m3"):
    dtype, down = {"e4m3": (ml_dtypes.float8_e4m3fn, 7), "e5m2": (ml_dtypes.float8_e5m2, 14)}[fmt]
    v = np.moveaxis(np.asarray(x, np.float32).astype(ml_dtypes.bfloat16).astype(np.float64), axis, -1)
    blocks = v.reshape(v.shape[:-1] + (-1, 32))
    amax = np.abs(blocks).max(-1, keepdims=True)
    byte = np.maximum(np.where(amax > 0, np.frexp(amax)[1] - 1 + 127, 0) - down, 1)
    scale = np.exp2(byte - 127.0)
    codes = (blocks / scale).astype(np.float32).astype(dtype).astype(np.float64)
    return np.moveaxis((codes * scale).reshape(v.shape), -1, axis)


WIDE = False


def mx_kscale(k):
    if not WIDE:
        return np.ones(k)
    levels = np.array([10, -10, 5, -5, 0])
    a = np.random.permutation(np.resize(levels, k // 512 * 4)).reshape(k // 512, 4)
    idx = np.arange(k)
    return np.exp2(a[idx // 512, idx % 128 // 32])


BF16 = ml_dtypes.bfloat16


def bf(x):
    return np.asarray(x, np.float32).astype(BF16)


def f64(x):
    return np.asarray(x).astype(np.float64)


SL, BS, DM, H, NH, DO = 32, 128, 1024, 16, 64, 1024
DP = H * NH


def log_softmax0(x):
    z = x - x.max(0, keepdims=True)
    return z - np.log(np.exp(z).sum(0, keepdims=True))


def setup_inputs():
    s, u = mx_kscale(DM), mx_kscale(DM)
    return {"query": bf(np.random.standard_normal((BS, DM)) * 2.0 * s),
            "keys": bf(np.random.standard_normal((SL, BS, DM)) * u),
            "Wq": bf(np.random.standard_normal((DP, DM)) / np.sqrt(DM) / s),
            "Wk": bf(np.random.standard_normal((DP, DM)) / np.sqrt(DM) / u)}


def reference(query, keys, Wq, Wk):
    qp = mxq(f64(query), 1, "e4m3") @ mxq(f64(Wq), 1, "e4m3").T
    kp = mxq(f64(keys), 2, "e4m3") @ mxq(f64(Wk), 1, "e4m3").T
    dot = (qp * kp).reshape(SL, BS, H, NH).sum(-1) / np.sqrt(NH)
    return log_softmax0(dot)

@@ -1,0 +1,194 @@
+from contextlib import ExitStack
+
+import concourse.mybir as mybir
+from concourse.masks import make_identity
+
+F32 = mybir.dt.float32
+BF16 = mybir.dt.bfloat16
+U32 = mybir.dt.uint32
+U8 = mybir.dt.uint8
+FP8X4 = mybir.dt.float8_e4m3fn_x4
+ALU = mybir.AluOpType
+ACT = mybir.ActivationFunctionType
+AXIS_X = mybir.AxisListType.X
+
+P = 128
+PACK = 4
+SEQ = 32
+FEAT = 1024
+HEADS = 16
+HEAD_DIM = 64
+CHAN = HEADS * HEAD_DIM
+PASSES = FEAT // (P * PACK)
+BANK = 512
+HALVES = CHAN // BANK
+BANK_HEADS = BANK // HEAD_DIM
+BANK_TILES = BANK // P
+ROUND = 2
+ROUNDS = SEQ // ROUND
+FOLD_WIDTHS = (32, 16, 8)
+
+FLOPS = 2 * (SEQ + 1) * P * FEAT * CHAN
+
+
+def tile_multiheadattention_pa_kernel(tc, query, keys, Wq, Wk, out):
+    nc = tc.nc
+    with ExitStack() as ctx:
+        ctx.enter_context(tc.manual_schedule())
+        raw = ctx.enter_context(tc.tile_pool(name="raw", bufs=1))
+        keep = ctx.enter_context(tc.tile_pool(name="keep", bufs=1))
+        stages = ctx.enter_context(tc.tile_pool(name="stages", bufs=3))
+        packed = ctx.enter_context(tc.tile_pool(name="packed", bufs=3))
+        prods = ctx.enter_context(tc.tile_pool(name="prods", bufs=6))
+        folds = ctx.enter_context(tc.tile_pool(name="folds", bufs=3))
+        scrap = ctx.enter_context(tc.tile_pool(name="scrap", bufs=2))
+        psum = ctx.enter_context(tc.psum_pool(name="psum", bufs=1))
+
+        query_raw = raw.tile([P, 1, FEAT], BF16)
+        nc.sync.dma_start(out=query_raw[:, 0, :], in_=query)
+        weight_raw = {}
+        for name, weight in (("wq", Wq), ("wk", Wk)):
+            for half in range(HALVES):
+                rows = raw.tile([P, BANK_TILES, FEAT], BF16, name="%s_raw%d" % (name, half))
+                nc.sync.dma_start(
+                    out=rows,
+                    in_=weight[half * BANK : (half + 1) * BANK, :].rearrange(
+                        "(t p) k -> p t k", p=P
+                    ),
+                )
+                weight_raw[(name, half)] = rows
+        keys_raw = []
+        for r in range(ROUNDS):
+            rows = raw.tile([P, ROUND, FEAT], BF16, name="keys_raw%d" % r)
+            nc.sync.dma_start(
+                out=rows, in_=keys[r * ROUND : (r + 1) * ROUND].rearrange("s b k -> b s k")
+            )
+            keys_raw.append(rows)
+
+        ident = keep.tile([P, P], F32)
+        make_identity(nc, ident)
+
+        warm = keep.tile([P, 1], F32)
+        nc.vector.memset(warm, 0.0)
+        nc.scalar.activation(out=warm, in_=warm, func=ACT.Exp)
+
+        def transpose_and_regroup(rows, bank_tag):
+            n = rows.shape[1]
+            stage = stages.tile([P, PASSES, n, P, PACK], BF16, align_bytes=64, tag="stage%d" % n)
+            stage_words = stage.bitcast(F32)
+            for i in range(n):
+                words = rows[:, i, :].bitcast(F32)
+                bank = psum.tile([P, PASSES, 2, P], F32, tag=bank_tag, name="bank", bufs=(2 if bank_tag == "xt" else 6))
+                for g in range(PASSES):
+                    for u in range(2):
+                        first = (2 * g + u) * P
+                        nc.tensor.transpose(bank[:, g, u, :], words[:, first : first + P], ident)
+                nc.scalar.copy(
+                    out=stage_words[:, :, i, :, :], in_=bank.rearrange("p g u r -> p g r u")
+                )
+            return stage
+
+        def quantise(stage, codes, scales):
+            nc.vector.quantize_mx(
+                out=codes.rearrange("p g i r -> p (g i r)").bitcast(FP8X4),
+                scales=scales.rearrange("p g i r -> p (g i r)"),
+                in_=stage.rearrange("p g i r t -> p (g i r t)"),
+            )
+
+        q_codes = keep.tile([P, PASSES, 1, P], U32, align_bytes=64)
+        q_scales = keep.tile([P, PASSES, 1, P], U8, align_bytes=64)
+        quantise(transpose_and_regroup(query_raw, "kp"), q_codes, q_scales)
+        w_codes = {}
+        w_scales = {}
+        for name in ("wq", "wk"):
+            for half in range(HALVES):
+                codes = keep.tile([P, PASSES, BANK_TILES, P], U32, align_bytes=64, name="%s_codes%d" % (name, half))
+                scales = keep.tile([P, PASSES, BANK_TILES, P], U8, align_bytes=64, name="%s_scales%d" % (name, half))
+                quantise(transpose_and_regroup(weight_raw[(name, half)], "kp"), codes, scales)
+                w_codes[(name, half)] = codes.rearrange("p g i r -> p g (i r)")
+                w_scales[(name, half)] = scales.rearrange("p g i r -> p g (i r)")
+
+        def project(bank, codes, scales, i, name, half):
+            for g in range(PASSES):
+                nc.tensor.matmul_mx(
+                    out=bank,
+                    lhsT=codes[:, g, i, :].bitcast(FP8X4),
+                    lhsT_scale=scales[:, g, i, :],
+                    rhs=w_codes[(name, half)][:, g, :].bitcast(FP8X4),
+                    rhs_scale=w_scales[(name, half)][:, g, :],
+                    start=(g == 0),
+                    stop=(g == PASSES - 1),
+                )
+
+        qp = keep.tile([P, HALVES, BANK_HEADS, HEAD_DIM], F32)
+        for half in range(HALVES):
+            qp_bank = psum.tile([P, BANK_HEADS, HEAD_DIM], F32, tag="kp", bufs=6)
+            project(qp_bank.rearrange("p h j -> p (h j)"), q_codes, q_scales, 0, "wq", half)
+            nc.scalar.activation(out=qp[:, half], in_=qp_bank, func=ACT.Copy, scale=HEAD_DIM**-0.5)
+
+        dot = keep.tile([P, SEQ, HEADS], F32)
+        key_stage = {}
+        key_codes = {}
+        key_scales = {}
+        products = {}
+        for r in range(-2, ROUNDS + 1):
+            if r + 2 < ROUNDS:
+                key_stage[r + 2] = transpose_and_regroup(keys_raw[r + 2], "xt")
+            if 0 <= r + 1 < ROUNDS:
+                codes = packed.tile([P, PASSES, ROUND, P], U32, align_bytes=64)
+                scales = packed.tile([P, PASSES, ROUND, P], U8, align_bytes=64)
+                quantise(key_stage[r + 1], codes, scales)
+                key_codes[r + 1] = codes
+                key_scales[r + 1] = scales
+            if 0 <= r < ROUNDS:
+                for i in range(ROUND):
+                    product = prods.tile([P, HALVES, BANK_HEADS, HEAD_DIM], F32)
+                    for half in range(HALVES):
+                        kp = psum.tile([P, BANK_HEADS, HEAD_DIM], F32, tag="kp", bufs=6)
+                        project(kp.rearrange("p h j -> p (h j)"), key_codes[r], key_scales[r], i, "wk", half)
+                        nc.vector.tensor_tensor(out=product[:, half], in0=kp, in1=qp[:, half], op=ALU.mult)
+                    products[(r, i)] = product.rearrange("p n h j -> p (n h) j")
+            if 0 <= r - 1:
+                for i in range(ROUND):
+                    s = (r - 1) * ROUND + i
+                    product = products[(r - 1, i)]
+                    if i % 2 == 0:
+                        for width in FOLD_WIDTHS:
+                            folded = folds.tile([P, HEADS, width], F32, tag="folded%d" % width)
+                            nc.gpsimd.tensor_tensor(
+                                out=folded,
+                                in0=product[:, :, 0:width],
+                                in1=product[:, :, width : 2 * width],
+                                op=ALU.add,
+                            )
+                            product = folded
+                        nc.vector.tensor_reduce(out=dot[:, s, :], in_=product, axis=AXIS_X, op=ALU.add)
+                    else:
+                        unread = scrap.tile([P, HEADS, HEAD_DIM], F32)
+                        for h in range(HEADS):
+                            nc.scalar.activation(
+                                out=unread[:, h, :],
+                                in_=product[:, h, :],
+                                func=ACT.Copy,
+                                accum_out=dot[:, s, h : h + 1],
+                            )
+
+        by_head = "p s h -> p h s"
+        top = keep.tile([P, HEADS], F32)
+        nc.vector.tensor_reduce(out=top, in_=dot.rearrange(by_head), axis=AXIS_X, op=ALU.max)
+        shifted = keep.tile([P, SEQ, HEADS], F32)
+        nc.vector.tensor_tensor(
+            out=shifted, in0=dot, in1=top.unsqueeze(1).to_broadcast([P, SEQ, HEADS]), op=ALU.subtract
+        )
+        grown = keep.tile([P, SEQ, HEADS], F32)
+        nc.scalar.activation(out=grown, in_=shifted, func=ACT.Exp)
+        nc.scalar.activation(out=warm, in_=warm, func=ACT.Ln)
+        total = keep.tile([P, HEADS], F32)
+        nc.vector.tensor_reduce(out=total, in_=grown.rearrange(by_head), axis=AXIS_X, op=ALU.add)
+        log_total = keep.tile([P, HEADS], F32)
+        nc.scalar.activation(out=log_total, in_=total, func=ACT.Ln)
+        result = keep.tile([P, SEQ, HEADS], F32)
+        nc.vector.tensor_tensor(
+            out=result, in0=shifted, in1=log_total.unsqueeze(1).to_broadcast([P, SEQ, HEADS]), op=ALU.subtract
+        )
+        nc.sync.dma_start(out=out.rearrange("s b h -> b s h"), in_=result)

@@ -134,20 +134,20 @@ def tile_multiheadattention_pa_kernel(tc, query, keys, Wq, Wk, out):
         for r in range(-2, ROUNDS + 1):
             if r + 2 < ROUNDS:
                 key_stage[r + 2] = transpose_and_regroup(keys_raw[r + 2], "xt")
-            if 0 <= r + 1 < ROUNDS:
-                codes = packed.tile([P, PASSES, ROUND, P], U32, align_bytes=64)
-                scales = packed.tile([P, PASSES, ROUND, P], U8, align_bytes=64)
-                quantise(key_stage[r + 1], codes, scales)
-                key_codes[r + 1] = codes
-                key_scales[r + 1] = scales
-            if 0 <= r < ROUNDS:
-                for i in range(ROUND):
+            for i in range(ROUND):
+                if 0 <= r < ROUNDS:
                     product = prods.tile([P, HALVES, BANK_HEADS, HEAD_DIM], F32)
                     for half in range(HALVES):
                         kp = psum.tile([P, BANK_HEADS, HEAD_DIM], F32, tag="kp", bufs=6)
                         project(kp.rearrange("p h j -> p (h j)"), key_codes[r], key_scales[r], i, "wk", half)
                         nc.vector.tensor_tensor(out=product[:, half], in0=kp, in1=qp[:, half], op=ALU.mult)
                     products[(r, i)] = product.rearrange("p n h j -> p (n h) j")
+                if i == 0 and 0 <= r + 1 < ROUNDS:
+                    codes = packed.tile([P, PASSES, ROUND, P], U32, align_bytes=64)
+                    scales = packed.tile([P, PASSES, ROUND, P], U8, align_bytes=64)
+                    quantise(key_stage[r + 1], codes, scales)
+                    key_codes[r + 1] = codes
+                    key_scales[r + 1] = scales
             if 0 <= r - 1:
                 for i in range(ROUND):
                     s = (r - 1) * ROUND + i

@@ -20,12 +20,14 @@ HEADS = 16
 HEAD_DIM = 64
 CHAN = HEADS * HEAD_DIM
 PASSES = FEAT // (P * PACK)
+ROUND = 2
+ROUNDS = SEQ // ROUND
+GROUP = ROUND * P
+GROUPS = CHAN // GROUP
 BANK = 512
 HALVES = CHAN // BANK
 BANK_HEADS = BANK // HEAD_DIM
-BANK_TILES = BANK // P
-ROUND = 2
-ROUNDS = SEQ // ROUND
+BANK_GROUPS = BANK // GROUP
 FOLD_WIDTHS = (32, 16, 8)
 
 FLOPS = 2 * (SEQ + 1) * P * FEAT * CHAN
@@ -37,7 +39,7 @@ def tile_multiheadattention_pa_kernel(tc, query, keys, Wq, Wk, out):
         ctx.enter_context(tc.manual_schedule())
         raw = ctx.enter_context(tc.tile_pool(name="raw", bufs=1))
         keep = ctx.enter_context(tc.tile_pool(name="keep", bufs=1))
-        stages = ctx.enter_context(tc.tile_pool(name="stages", bufs=3))
+        stages = ctx.enter_context(tc.tile_pool(name="stages", bufs=4))
         packed = ctx.enter_context(tc.tile_pool(name="packed", bufs=3))
         prods = ctx.enter_context(tc.tile_pool(name="prods", bufs=6))
         folds = ctx.enter_context(tc.tile_pool(name="folds", bufs=3))
@@ -48,15 +50,13 @@ def tile_multiheadattention_pa_kernel(tc, query, keys, Wq, Wk, out):
         nc.sync.dma_start(out=query_raw[:, 0, :], in_=query)
         weight_raw = {}
         for name, weight in (("wq", Wq), ("wk", Wk)):
-            for half in range(HALVES):
-                rows = raw.tile([P, BANK_TILES, FEAT], BF16, name="%s_raw%d" % (name, half))
+            for c in range(GROUPS):
+                rows = raw.tile([P, ROUND, FEAT], BF16, name="%s_raw%d" % (name, c))
                 nc.sync.dma_start(
                     out=rows,
-                    in_=weight[half * BANK : (half + 1) * BANK, :].rearrange(
-                        "(t p) k -> p t k", p=P
-                    ),
+                    in_=weight[c * GROUP : (c + 1) * GROUP, :].rearrange("(i p) k -> p i k", p=P),
                 )
-                weight_raw[(name, half)] = rows
+                weight_raw[(name, c)] = rows
         keys_raw = []
         for r in range(ROUNDS):
             rows = raw.tile([P, ROUND, FEAT], BF16, name="keys_raw%d" % r)
@@ -72,82 +72,84 @@ def tile_multiheadattention_pa_kernel(tc, query, keys, Wq, Wk, out):
         nc.vector.memset(warm, 0.0)
         nc.scalar.activation(out=warm, in_=warm, func=ACT.Exp)
 
-        def transpose_and_regroup(rows, bank_tag):
+        def transpose_and_regroup(rows, bank_tag, bank_bufs, vector_helps):
             n = rows.shape[1]
             stage = stages.tile([P, PASSES, n, P, PACK], BF16, align_bytes=64, tag="stage%d" % n)
             stage_words = stage.bitcast(F32)
             for i in range(n):
                 words = rows[:, i, :].bitcast(F32)
-                bank = psum.tile([P, PASSES, 2, P], F32, tag=bank_tag, name="bank", bufs=(2 if bank_tag == "xt" else 6))
+                bank = psum.tile([P, PASSES, 2, P], F32, tag=bank_tag, bufs=bank_bufs)
                 for g in range(PASSES):
                     for u in range(2):
                         first = (2 * g + u) * P
                         nc.tensor.transpose(bank[:, g, u, :], words[:, first : first + P], ident)
-                nc.scalar.copy(
-                    out=stage_words[:, :, i, :, :], in_=bank.rearrange("p g u r -> p g r u")
-                )
+                if vector_helps and i % 2 == 1:
+                    nc.vector.tensor_copy(
+                        out=stage_words[:, :, i, :, :], in_=bank.rearrange("p g u r -> p g r u")
+                    )
+                else:
+                    nc.scalar.copy(
+                        out=stage_words[:, :, i, :, :], in_=bank.rearrange("p g u r -> p g r u")
+                    )
             return stage
 
-        def quantise(stage, codes, scales):
+        def quantise(stage, pool, name):
+            n = stage.shape[2]
+            codes = pool.tile([P, PASSES, n, P], U32, align_bytes=64, name="%s_codes" % name)
+            scales = pool.tile([P, PASSES, n, P], U8, align_bytes=64, name="%s_scales" % name)
             nc.vector.quantize_mx(
                 out=codes.rearrange("p g i r -> p (g i r)").bitcast(FP8X4),
                 scales=scales.rearrange("p g i r -> p (g i r)"),
                 in_=stage.rearrange("p g i r t -> p (g i r t)"),
             )
+            return codes, scales
 
-        q_codes = keep.tile([P, PASSES, 1, P], U32, align_bytes=64)
-        q_scales = keep.tile([P, PASSES, 1, P], U8, align_bytes=64)
-        quantise(transpose_and_regroup(query_raw, "kp"), q_codes, q_scales)
-        w_codes = {}
-        w_scales = {}
+        q_mx = quantise(transpose_and_regroup(query_raw, "kp", 6, False), keep, "q")
+        w_mx = {}
         for name in ("wq", "wk"):
-            for half in range(HALVES):
-                codes = keep.tile([P, PASSES, BANK_TILES, P], U32, align_bytes=64, name="%s_codes%d" % (name, half))
-                scales = keep.tile([P, PASSES, BANK_TILES, P], U8, align_bytes=64, name="%s_scales%d" % (name, half))
-                quantise(transpose_and_regroup(weight_raw[(name, half)], "kp"), codes, scales)
-                w_codes[(name, half)] = codes.rearrange("p g i r -> p g (i r)")
-                w_scales[(name, half)] = scales.rearrange("p g i r -> p g (i r)")
+            for c in range(GROUPS):
+                stage = transpose_and_regroup(weight_raw[(name, c)], "kp", 6, False)
+                w_mx[(name, c)] = quantise(stage, keep, "%s%d" % (name, c))
 
-        def project(bank, codes, scales, i, name, half):
-            for g in range(PASSES):
-                nc.tensor.matmul_mx(
-                    out=bank,
-                    lhsT=codes[:, g, i, :].bitcast(FP8X4),
-                    lhsT_scale=scales[:, g, i, :],
-                    rhs=w_codes[(name, half)][:, g, :].bitcast(FP8X4),
-                    rhs_scale=w_scales[(name, half)][:, g, :],
-                    start=(g == 0),
-                    stop=(g == PASSES - 1),
-                )
+        def project(bank, rows_mx, i, name, half):
+            codes, scales = rows_mx
+            for c in range(BANK_GROUPS):
+                w_codes, w_scales = w_mx[(name, half * BANK_GROUPS + c)]
+                for g in range(PASSES):
+                    nc.tensor.matmul_mx(
+                        out=bank[:, c * GROUP : (c + 1) * GROUP],
+                        lhsT=codes[:, g, i, :].bitcast(FP8X4),
+                        lhsT_scale=scales[:, g, i, :],
+                        rhs=w_codes[:, g].rearrange("p i r -> p (i r)").bitcast(FP8X4),
+                        rhs_scale=w_scales[:, g].rearrange("p i r -> p (i r)"),
+                        start=(g == 0),
+                        stop=(g == PASSES - 1),
+                    )
 
         qp = keep.tile([P, HALVES, BANK_HEADS, HEAD_DIM], F32)
         for half in range(HALVES):
             qp_bank = psum.tile([P, BANK_HEADS, HEAD_DIM], F32, tag="kp", bufs=6)
-            project(qp_bank.rearrange("p h j -> p (h j)"), q_codes, q_scales, 0, "wq", half)
-            nc.scalar.activation(out=qp[:, half], in_=qp_bank, func=ACT.Copy, scale=HEAD_DIM**-0.5)
+            project(qp_bank.rearrange("p h j -> p (h j)"), q_mx, 0, "wq", half)
+            if half % 2 == 1:
+                nc.vector.tensor_scalar_mul(out=qp[:, half], in0=qp_bank, scalar1=HEAD_DIM**-0.5)
+            else:
+                nc.scalar.activation(out=qp[:, half], in_=qp_bank, func=ACT.Copy, scale=HEAD_DIM**-0.5)
 
         dot = keep.tile([P, SEQ, HEADS], F32)
         key_stage = {}
-        key_codes = {}
-        key_scales = {}
+        key_mx = {}
         products = {}
         for r in range(-2, ROUNDS + 1):
-            if r + 2 < ROUNDS:
-                key_stage[r + 2] = transpose_and_regroup(keys_raw[r + 2], "xt")
-            for i in range(ROUND):
-                if 0 <= r < ROUNDS:
+            if 0 <= r + 1 < ROUNDS:
+                key_mx[r + 1] = quantise(key_stage[r + 1], packed, "key")
+            if 0 <= r < ROUNDS:
+                for i in range(ROUND):
                     product = prods.tile([P, HALVES, BANK_HEADS, HEAD_DIM], F32)
                     for half in range(HALVES):
                         kp = psum.tile([P, BANK_HEADS, HEAD_DIM], F32, tag="kp", bufs=6)
-                        project(kp.rearrange("p h j -> p (h j)"), key_codes[r], key_scales[r], i, "wk", half)
+                        project(kp.rearrange("p h j -> p (h j)"), key_mx[r], i, "wk", half)
                         nc.vector.tensor_tensor(out=product[:, half], in0=kp, in1=qp[:, half], op=ALU.mult)
                     products[(r, i)] = product.rearrange("p n h j -> p (n h) j")
-                if i == 0 and 0 <= r + 1 < ROUNDS:
-                    codes = packed.tile([P, PASSES, ROUND, P], U32, align_bytes=64)
-                    scales = packed.tile([P, PASSES, ROUND, P], U8, align_bytes=64)
-                    quantise(key_stage[r + 1], codes, scales)
-                    key_codes[r + 1] = codes
-                    key_scales[r + 1] = scales
             if 0 <= r - 1:
                 for i in range(ROUND):
                     s = (r - 1) * ROUND + i
@@ -172,6 +174,8 @@ def tile_multiheadattention_pa_kernel(tc, query, keys, Wq, Wk, out):
                                 func=ACT.Copy,
                                 accum_out=dot[:, s, h : h + 1],
                             )
+            if r + 2 < ROUNDS:
+                key_stage[r + 2] = transpose_and_regroup(keys_raw[r + 2], "xt", 2, r < 0)
 
         by_head = "p s h -> p h s"
         top = keep.tile([P, HEADS], F32)
@@ -188,7 +192,15 @@ def tile_multiheadattention_pa_kernel(tc, query, keys, Wq, Wk, out):
         log_total = keep.tile([P, HEADS], F32)
         nc.scalar.activation(out=log_total, in_=total, func=ACT.Ln)
         result = keep.tile([P, SEQ, HEADS], F32)
-        nc.vector.tensor_tensor(
-            out=result, in0=shifted, in1=log_total.unsqueeze(1).to_broadcast([P, SEQ, HEADS]), op=ALU.subtract
-        )
-        nc.sync.dma_start(out=out.rearrange("s b h -> b s h"), in_=result)
+        part = SEQ // 2
+        for first, queue in ((0, nc.sync), (part, nc.scalar)):
+            nc.vector.tensor_tensor(
+                out=result[:, first : first + part, :],
+                in0=shifted[:, first : first + part, :],
+                in1=log_total.unsqueeze(1).to_broadcast([P, part, HEADS]),
+                op=ALU.subtract,
+            )
+            queue.dma_start(
+                out=out[first : first + part].rearrange("s b h -> b s h"),
+                in_=result[:, first : first + part, :],
+            )

from contextlib import ExitStack

import concourse.mybir as mybir
from concourse.masks import make_identity

F32 = mybir.dt.float32
BF16 = mybir.dt.bfloat16
U32 = mybir.dt.uint32
U8 = mybir.dt.uint8
FP8X4 = mybir.dt.float8_e4m3fn_x4
ALU = mybir.AluOpType
ACT = mybir.ActivationFunctionType
AXIS_X = mybir.AxisListType.X

P = 128
PACK = 4
SEQ = 32
FEAT = 1024
HEADS = 16
HEAD_DIM = 64
CHAN = HEADS * HEAD_DIM
PASSES = FEAT // (P * PACK)
ROUND = 2
ROUNDS = SEQ // ROUND
GROUP = ROUND * P
GROUPS = CHAN // GROUP
BANK = 512
HALVES = CHAN // BANK
BANK_HEADS = BANK // HEAD_DIM
BANK_GROUPS = BANK // GROUP
FOLD_WIDTHS = (32, 16, 8)

FLOPS = 2 * (SEQ + 1) * P * FEAT * CHAN


def tile_multiheadattention_pa_kernel(tc, query, keys, Wq, Wk, out):
    nc = tc.nc
    with ExitStack() as ctx:
        ctx.enter_context(tc.manual_schedule())
        raw = ctx.enter_context(tc.tile_pool(name="raw", bufs=1))
        keep = ctx.enter_context(tc.tile_pool(name="keep", bufs=1))
        stages = ctx.enter_context(tc.tile_pool(name="stages", bufs=4))
        packed = ctx.enter_context(tc.tile_pool(name="packed", bufs=3))
        prods = ctx.enter_context(tc.tile_pool(name="prods", bufs=6))
        folds = ctx.enter_context(tc.tile_pool(name="folds", bufs=3))
        scrap = ctx.enter_context(tc.tile_pool(name="scrap", bufs=2))
        psum = ctx.enter_context(tc.psum_pool(name="psum", bufs=1))

        query_raw = raw.tile([P, 1, FEAT], BF16)
        nc.sync.dma_start(out=query_raw[:, 0, :], in_=query)
        weight_raw = {}
        for name, weight in (("wq", Wq), ("wk", Wk)):
            for c in range(GROUPS):
                rows = raw.tile([P, ROUND, FEAT], BF16, name="%s_raw%d" % (name, c))
                nc.sync.dma_start(
                    out=rows,
                    in_=weight[c * GROUP : (c + 1) * GROUP, :].rearrange("(i p) k -> p i k", p=P),
                )
                weight_raw[(name, c)] = rows
        keys_raw = []
        for r in range(ROUNDS):
            rows = raw.tile([P, ROUND, FEAT], BF16, name="keys_raw%d" % r)
            nc.sync.dma_start(
                out=rows, in_=keys[r * ROUND : (r + 1) * ROUND].rearrange("s b k -> b s k")
            )
            keys_raw.append(rows)

        ident = keep.tile([P, P], F32)
        make_identity(nc, ident)

        warm = keep.tile([P, 1], F32)
        nc.vector.memset(warm, 0.0)
        nc.scalar.activation(out=warm, in_=warm, func=ACT.Exp)

        def transpose_and_regroup(rows, bank_tag, bank_bufs, vector_helps):
            n = rows.shape[1]
            stage = stages.tile([P, PASSES, n, P, PACK], BF16, align_bytes=64, tag="stage%d" % n)
            stage_words = stage.bitcast(F32)
            for i in range(n):
                words = rows[:, i, :].bitcast(F32)
                bank = psum.tile([P, PASSES, 2, P], F32, tag=bank_tag, bufs=bank_bufs)
                for g in range(PASSES):
                    for u in range(2):
                        first = (2 * g + u) * P
                        nc.tensor.transpose(bank[:, g, u, :], words[:, first : first + P], ident)
                if vector_helps and i % 2 == 1:
                    nc.vector.tensor_copy(
                        out=stage_words[:, :, i, :, :], in_=bank.rearrange("p g u r -> p g r u")
                    )
                else:
                    nc.scalar.copy(
                        out=stage_words[:, :, i, :, :], in_=bank.rearrange("p g u r -> p g r u")
                    )
            return stage

        def quantise(stage, pool, name):
            n = stage.shape[2]
            codes = pool.tile([P, PASSES, n, P], U32, align_bytes=64, name="%s_codes" % name)
            scales = pool.tile([P, PASSES, n, P], U8, align_bytes=64, name="%s_scales" % name)
            nc.vector.quantize_mx(
                out=codes.rearrange("p g i r -> p (g i r)").bitcast(FP8X4),
                scales=scales.rearrange("p g i r -> p (g i r)"),
                in_=stage.rearrange("p g i r t -> p (g i r t)"),
            )
            return codes, scales

        q_mx = quantise(transpose_and_regroup(query_raw, "kp", 6, False), keep, "q")
        w_mx = {}
        for name in ("wq", "wk"):
            for c in range(GROUPS):
                stage = transpose_and_regroup(weight_raw[(name, c)], "kp", 6, False)
                w_mx[(name, c)] = quantise(stage, keep, "%s%d" % (name, c))

        def project(bank, rows_mx, i, name, half):
            codes, scales = rows_mx
            for c in range(BANK_GROUPS):
                w_codes, w_scales = w_mx[(name, half * BANK_GROUPS + c)]
                for g in range(PASSES):
                    nc.tensor.matmul_mx(
                        out=bank[:, c * GROUP : (c + 1) * GROUP],
                        lhsT=codes[:, g, i, :].bitcast(FP8X4),
                        lhsT_scale=scales[:, g, i, :],
                        rhs=w_codes[:, g].rearrange("p i r -> p (i r)").bitcast(FP8X4),
                        rhs_scale=w_scales[:, g].rearrange("p i r -> p (i r)"),
                        start=(g == 0),
                        stop=(g == PASSES - 1),
                    )

        qp = keep.tile([P, HALVES, BANK_HEADS, HEAD_DIM], F32)
        for half in range(HALVES):
            qp_bank = psum.tile([P, BANK_HEADS, HEAD_DIM], F32, tag="kp", bufs=6)
            project(qp_bank.rearrange("p h j -> p (h j)"), q_mx, 0, "wq", half)
            if half % 2 == 1:
                nc.vector.tensor_scalar_mul(out=qp[:, half], in0=qp_bank, scalar1=HEAD_DIM**-0.5)
            else:
                nc.scalar.activation(out=qp[:, half], in_=qp_bank, func=ACT.Copy, scale=HEAD_DIM**-0.5)

        dot = keep.tile([P, SEQ, HEADS], F32)
        key_stage = {}
        key_mx = {}
        products = {}
        for r in range(-2, ROUNDS + 1):
            if 0 <= r + 1 < ROUNDS:
                key_mx[r + 1] = quantise(key_stage[r + 1], packed, "key")
            if 0 <= r < ROUNDS:
                for i in range(ROUND):
                    product = prods.tile([P, HALVES, BANK_HEADS, HEAD_DIM], F32)
                    for half in range(HALVES):
                        kp = psum.tile([P, BANK_HEADS, HEAD_DIM], F32, tag="kp", bufs=6)
                        project(kp.rearrange("p h j -> p (h j)"), key_mx[r], i, "wk", half)
                        nc.vector.tensor_tensor(out=product[:, half], in0=kp, in1=qp[:, half], op=ALU.mult)
                    products[(r, i)] = product.rearrange("p n h j -> p (n h) j")
            if 0 <= r - 1:
                for i in range(ROUND):
                    s = (r - 1) * ROUND + i
                    product = products[(r - 1, i)]
                    if i % 2 == 0:
                        for width in FOLD_WIDTHS:
                            folded = folds.tile([P, HEADS, width], F32, tag="folded%d" % width)
                            nc.gpsimd.tensor_tensor(
                                out=folded,
                                in0=product[:, :, 0:width],
                                in1=product[:, :, width : 2 * width],
                                op=ALU.add,
                            )
                            product = folded
                        nc.vector.tensor_reduce(out=dot[:, s, :], in_=product, axis=AXIS_X, op=ALU.add)
                    else:
                        unread = scrap.tile([P, HEADS, HEAD_DIM], F32)
                        for h in range(HEADS):
                            nc.scalar.activation(
                                out=unread[:, h, :],
                                in_=product[:, h, :],
                                func=ACT.Copy,
                                accum_out=dot[:, s, h : h + 1],
                            )
            if r + 2 < ROUNDS:
                key_stage[r + 2] = transpose_and_regroup(keys_raw[r + 2], "xt", 2, r < 0)

        by_head = "p s h -> p h s"
        top = keep.tile([P, HEADS], F32)
        nc.vector.tensor_reduce(out=top, in_=dot.rearrange(by_head), axis=AXIS_X, op=ALU.max)
        shifted = keep.tile([P, SEQ, HEADS], F32)
        nc.vector.tensor_tensor(
            out=shifted, in0=dot, in1=top.unsqueeze(1).to_broadcast([P, SEQ, HEADS]), op=ALU.subtract
        )
        grown = keep.tile([P, SEQ, HEADS], F32)
        nc.scalar.activation(out=grown, in_=shifted, func=ACT.Exp)
        nc.scalar.activation(out=warm, in_=warm, func=ACT.Ln)
        total = keep.tile([P, HEADS], F32)
        nc.vector.tensor_reduce(out=total, in_=grown.rearrange(by_head), axis=AXIS_X, op=ALU.add)
        log_total = keep.tile([P, HEADS], F32)
        nc.scalar.activation(out=log_total, in_=total, func=ACT.Ln)
        result = keep.tile([P, SEQ, HEADS], F32)
        part = SEQ // 2
        for first, queue in ((0, nc.sync), (part, nc.scalar)):
            nc.vector.tensor_tensor(
                out=result[:, first : first + part, :],
                in0=shifted[:, first : first + part, :],
                in1=log_total.unsqueeze(1).to_broadcast([P, part, HEADS]),
                op=ALU.subtract,
            )
            queue.dma_start(
                out=out[first : first + part].rearrange("s b h -> b s h"),
                in_=result[:, first : first + part, :],
            )
